import numpy as np
import ml_dtypes


def mxq(x, axis, fmt="e4m3"):
    dtype, down = {"e4m3": (ml_dtypes.float8_e4m3fn, 7), "e5m2": (ml_dtypes.float8_e5m2, 14)}[fmt]
    v = np.moveaxis(np.asarray(x, np.float32).astype(ml_dtypes.bfloat16).astype(np.float64), axis, -1)
    blocks = v.reshape(v.shape[:-1] + (-1, 32))
    amax = np.abs(blocks).max(-1, keepdims=True)
    byte = np.maximum(np.where(amax > 0, np.frexp(amax)[1] - 1 + 127, 0) - down, 1)
    scale = np.exp2(byte - 127.0)
    codes = (blocks / scale).astype(np.float32).astype(dtype).astype(np.float64)
    return np.moveaxis((codes * scale).reshape(v.shape), -1, axis)


WIDE = False


def mx_kscale(k):
    if not WIDE:
        return np.ones(k)
    levels = np.array([10, -10, 5, -5, 0])
    if k % 512:
        return np.exp2(np.random.permutation(np.resize(levels, k // 32))).repeat(32)
    a = np.empty((k // 512, 16))
    for p in range(k // 512):
        a[p, :8] = np.random.permutation(np.resize(levels, 8))
        for g in range(8):
            far = levels[np.abs(levels - a[p, g]) >= 10]
            a[p, g + 8] = far[np.random.randint(len(far))]
    return np.exp2(a.ravel()).repeat(32)


BF16 = ml_dtypes.bfloat16


def bf(x):
    return np.asarray(x, np.float32).astype(BF16)


def f64(x):
    return np.asarray(x).astype(np.float64)


B, L, D, F, K = 128, 8, 128, 1024, 16
EPS = 1e-12


def silu(v):
    return v / (1.0 + np.exp(-v))


def l2norm(t, axis):
    n = np.sqrt((t * t).sum(axis=axis, keepdims=True))
    return t / np.maximum(n, EPS)


def mix_draw(rows, cols):
    return np.random.standard_normal((L, rows, cols)) * np.sqrt(np.e / K) * np.exp(0.5 * np.random.standard_normal((L, 1, cols)))


def hidden_draw():
    return silu(3.0 * np.random.standard_normal((B, L, F))) * np.random.standard_normal((B, L, F)) * 3.0 / np.sqrt(D)


def setup_inputs():
    t = mx_kscale(F)
    g = np.sqrt(np.mean(1.0 / t**2))
    return {"h": bf(hidden_draw() * t * g),
            "w_down_mix": bf(mix_draw(F, D) / t[:, None])}


def reference(h, w_down_mix):
    wd = l2norm(f64(w_down_mix), 1)
    y = mxq(f64(h).transpose(1, 0, 2), 2, "e4m3") @ mxq(wd, 1, "e4m3")
    return l2norm(y, -1).transpose(1, 0, 2)

@@ -1,0 +1,204 @@
+import concourse.mybir as mybir
+from concourse.masks import make_identity
+
+F32 = mybir.dt.float32
+BF16 = mybir.dt.bfloat16
+U32 = mybir.dt.uint32
+U8 = mybir.dt.uint8
+FP8X4 = mybir.dt.float8_e4m3fn_x4
+ACT = mybir.ActivationFunctionType
+ALU = mybir.AluOpType
+
+P = 128
+B, L, F, D = 128, 8, 1024, 128
+PACK = 4
+PASSES = F // (P * PACK)
+ROWS = F // P
+HALVES = 2
+EPS = 1e-12
+
+FLOPS = 2 * B * L * F * D
+
+H_COPIES_ON_VECTOR = 2
+BANK_TOKENS = 4
+PAIR = 2
+RUN = 4
+
+
+def tile_npertokenswishglu_basis_pb_s_kernel(tc, h, w_down_mix, out):
+    nc = tc.nc
+    with tc.tile_pool(name="keep", bufs=1) as keep, tc.psum_pool(
+        name="wt_psum", bufs=2
+    ) as wt_psum, tc.psum_pool(name="ht_psum", bufs=2) as ht_psum, tc.psum_pool(
+        name="scale_psum", bufs=2
+    ) as scale_psum, tc.psum_pool(name="y_psum", bufs=2) as y_psum, tc.manual_schedule():
+        w_sb = keep.tile([P, L, ROWS, D], BF16)
+        h_sb = keep.tile([P, L, F], BF16)
+        for l in range(L):
+            nc.sync.dma_start(
+                out=w_sb[:, l].rearrange("p (g t) j -> p g (t j)", t=PACK),
+                in_=w_down_mix[l].rearrange("(g p t) j -> p g (t j)", p=P, t=PACK),
+            )
+            nc.sync.dma_start(out=h_sb[:, l, :], in_=h[:, l, :])
+        h_words = h_sb[:].bitcast(F32)
+
+        ident_bf = keep.tile([P, P], BF16)
+        make_identity(nc, ident_bf[:])
+        ident_f32 = keep.tile([P, P], F32)
+        make_identity(nc, ident_f32[:])
+
+        one = keep.tile([P, 1], F32)
+        nc.vector.memset(one[:], 1.0)
+        warm = keep.tile([P, 1], F32)
+        nc.scalar.activation(out=warm[:], in_=one[:], func=ACT.Abs_reciprocal_sqrt)
+
+        w_squares = keep.tile([P, L, ROWS, P], BF16)
+        w_sumsq = keep.tile([P, L, ROWS // RUN], F32)
+        w_rsqrt = keep.tile([P, L], F32)
+        nd_grouped = keep.tile([P, L, PASSES, D, PACK], BF16, align_bytes=64)
+        nd_codes = keep.tile([P, L, PASSES, D], U32, align_bytes=64)
+        nd_scales = keep.tile([P, L, PASSES, D], U8, align_bytes=64)
+        h_grouped = keep.tile([P, L, PASSES, B, PACK], BF16, align_bytes=64)
+        h_codes = keep.tile([P, L, PASSES, B], U32, align_bytes=64)
+        h_scales = keep.tile([P, L, PASSES, B], U8, align_bytes=64)
+        y_squares = keep.tile([P, L, D], F32)
+        y_sumsq = keep.tile([P, L], F32)
+        y_rsqrt = keep.tile([P, L], F32)
+        out_sb = keep.tile([P, L, D], F32)
+        w_rsqrt_spread = {}
+        y_banks = {}
+
+
+        def transpose_h(l):
+            hT = ht_psum.tile([P, PASSES, HALVES, B], F32)
+            for g in range(PASSES):
+                for u in range(HALVES):
+                    words = h_words[:, l, g * HALVES * P + u : (g + 1) * HALVES * P : HALVES]
+                    nc.tensor.transpose(hT[:, g, u, :], words, ident_f32[:])
+            grouped_words = h_grouped[:, l].bitcast(F32)
+            if l < H_COPIES_ON_VECTOR:
+                nc.vector.tensor_copy(out=grouped_words, in_=hT[:].rearrange("p g u b -> p g b u"))
+            else:
+                nc.scalar.copy(out=grouped_words, in_=hT[:].rearrange("p g u b -> p g b u"))
+
+        def sum_weight_squares(l):
+            for run in range(ROWS // RUN):
+                wT = wt_psum.tile([P, RUN, P], BF16)
+                for i in range(RUN):
+                    nc.tensor.transpose(wT[:, i, :], w_sb[:, l, run * RUN + i, :], ident_bf[:])
+                nc.scalar.activation(
+                    out=w_squares[:, l, run * RUN : (run + 1) * RUN],
+                    in_=wT[:],
+                    func=ACT.Square,
+                    accum_out=w_sumsq[:, l, run : run + 1],
+                )
+
+        def weight_rsqrt(l):
+            nc.scalar.activation(
+                out=w_rsqrt[:, l : l + 1],
+                in_=w_sumsq[:, l, 0:1],
+                func=ACT.Abs_reciprocal_sqrt,
+                bias=w_sumsq[:, l, 1:2],
+            )
+
+        def spread_weight_rsqrt(l):
+            w_rsqrt_spread[l] = scale_psum.tile([P, D], F32, name="w_rsqrt_spread")
+            nc.tensor.transpose(
+                w_rsqrt_spread[l][:], w_rsqrt[:, l : l + 1].to_broadcast([P, P]), ident_f32[:]
+            )
+
+        def scale_weight(l):
+            for g in range(PASSES):
+                nc.vector.scalar_tensor_tensor(
+                    out=nd_grouped[:, l, g],
+                    in0=w_rsqrt_spread[l][:].unsqueeze(2).to_broadcast([P, D, PACK]),
+                    scalar=1.0 / EPS,
+                    in1=w_sb[:, l, g * PACK : (g + 1) * PACK, :].rearrange("p t j -> p j t"),
+                    op0=ALU.min,
+                    op1=ALU.mult,
+                )
+
+        def quantise_h(l):
+            nc.vector.quantize_mx(
+                out=h_codes[:, l].rearrange("p g b -> p (g b)").bitcast(FP8X4),
+                scales=h_scales[:, l].rearrange("p g b -> p (g b)"),
+                in_=h_grouped[:, l].rearrange("p g b t -> p (g b t)"),
+            )
+
+        def quantise_nd(l):
+            nc.vector.quantize_mx(
+                out=nd_codes[:, l].rearrange("p g j -> p (g j)").bitcast(FP8X4),
+                scales=nd_scales[:, l].rearrange("p g j -> p (g j)"),
+                in_=nd_grouped[:, l].rearrange("p g j t -> p (g j t)"),
+            )
+
+        def multiply(l):
+            if l % BANK_TOKENS == 0:
+                y_banks[l // BANK_TOKENS] = y_psum.tile([P, BANK_TOKENS, D], F32, name="y_bank")
+            for g in range(PASSES):
+                nc.tensor.matmul_mx(
+                    out=y_banks[l // BANK_TOKENS][:, l % BANK_TOKENS, :],
+                    lhsT=h_codes[:, l, g, :].bitcast(FP8X4),
+                    lhsT_scale=h_scales[:, l, g, :],
+                    rhs=nd_codes[:, l, g, :].bitcast(FP8X4),
+                    rhs_scale=nd_scales[:, l, g, :],
+                    start=(g == 0),
+                    stop=(g == PASSES - 1),
+                )
+
+        def sum_row_squares(l):
+            nc.scalar.activation(
+                out=y_squares[:, l, :],
+                in_=y_banks[l // BANK_TOKENS][:, l % BANK_TOKENS, :],
+                func=ACT.Square,
+                accum_out=y_sumsq[:, l : l + 1],
+            )
+
+        def row_rsqrt(ls):
+            nc.scalar.activation(
+                out=y_rsqrt[:, ls], in_=y_sumsq[:, ls], func=ACT.Abs_reciprocal_sqrt
+            )
+
+        def normalise_and_store(first):
+            ls = slice(first, first + PAIR)
+            in_bank = first % BANK_TOKENS
+            nc.vector.scalar_tensor_tensor(
+                out=out_sb[:, ls, :],
+                in0=y_rsqrt[:, ls].unsqueeze(2).to_broadcast([P, PAIR, D]),
+                scalar=1.0 / EPS,
+                in1=y_banks[first // BANK_TOKENS][:, in_bank : in_bank + PAIR, :],
+                op0=ALU.min,
+                op1=ALU.mult,
+            )
+            nc.sync.dma_start(out=out[:, ls, :], in_=out_sb[:, ls, :])
+
+        def when_in_range(stage, l):
+            if 0 <= l < L:
+                stage(l)
+
+        def when_pair_complete(stage, l):
+            if 0 <= l < L and l % PAIR == PAIR - 1:
+                stage(l)
+
+        def multiply_pair(l):
+            multiply(l - 1)
+            multiply(l)
+
+        def row_rsqrt_pair(l):
+            row_rsqrt(slice(l - 1, l + 1))
+
+        def normalise_and_store_pair(l):
+            normalise_and_store(l - 1)
+
+        for step in range(L + 9):
+            when_in_range(spread_weight_rsqrt, step - 2)
+            when_in_range(sum_weight_squares, step)
+            when_in_range(transpose_h, step)
+            when_in_range(weight_rsqrt, step)
+            when_pair_complete(row_rsqrt_pair, step - 6)
+            when_in_range(scale_weight, step - 2)
+            when_in_range(quantise_h, step - 1)
+            when_in_range(quantise_nd, step - 2)
+            when_pair_complete(multiply_pair, step - 4)
+            when_in_range(sum_row_squares, step - 5)
+            when_pair_complete(normalise_and_store_pair, step - 8)

@@ -21,6 +21,7 @@ FLOPS = 2 * B * L * F * D
 
 H_COPIES_ON_VECTOR = 2
 BANK_TOKENS = 4
+SPREAD_BY_MATMUL = 6
 PAIR = 2
 RUN = 4
 
@@ -103,9 +104,13 @@ def tile_npertokenswishglu_basis_pb_s_kernel(tc, h, w_down_mix, out):
 
         def spread_weight_rsqrt(l):
             w_rsqrt_spread[l] = scale_psum.tile([P, D], F32, name="w_rsqrt_spread")
-            nc.tensor.transpose(
-                w_rsqrt_spread[l][:], w_rsqrt[:, l : l + 1].to_broadcast([P, P]), ident_f32[:]
-            )
+            column = w_rsqrt[:, l : l + 1].to_broadcast([P, P])
+            if l < SPREAD_BY_MATMUL:
+                nc.tensor.matmul(
+                    w_rsqrt_spread[l][:], lhsT=column, rhs=ident_f32[:], start=True, stop=True
+                )
+            else:
+                nc.tensor.transpose(w_rsqrt_spread[l][:], column, ident_f32[:])
 
         def scale_weight(l):
             for g in range(PASSES):

@@ -20,10 +20,11 @@ EPS = 1e-12
 FLOPS = 2 * B * L * F * D
 
 H_COPIES_ON_VECTOR = 2
-BANK_TOKENS = 4
-SPREAD_BY_MATMUL = 6
+SPREAD_BY_PRODUCT = 6
 PAIR = 2
-RUN = 4
+ALONE = L - PAIR
+PAIRS = D // 2
+BLOCKS = ROWS // 2
 
 
 def tile_npertokenswishglu_basis_pb_s_kernel(tc, h, w_down_mix, out):
@@ -43,19 +44,28 @@ def tile_npertokenswishglu_basis_pb_s_kernel(tc, h, w_down_mix, out):
             nc.sync.dma_start(out=h_sb[:, l, :], in_=h[:, l, :])
         h_words = h_sb[:].bitcast(F32)
 
-        ident_bf = keep.tile([P, P], BF16)
-        make_identity(nc, ident_bf[:])
+        w_words = w_sb[:].rearrange("p l r j -> p l (r j)").bitcast(F32)
+
         ident_f32 = keep.tile([P, P], F32)
         make_identity(nc, ident_f32[:])
+        fold = keep.tile([P, PAIRS], F32)
+        nc.vector.tensor_tensor(
+            out=fold[:], in0=ident_f32[:, :PAIRS], in1=ident_f32[:, PAIRS:], op=ALU.add
+        )
+        place = keep.tile([P, 2, PAIRS, 2], F32)
+        nc.vector.memset(place[:], 0.0)
+        for e in range(2):
+            nc.vector.tensor_copy(out=place[:, e, :, e], in_=fold[:])
 
         one = keep.tile([P, 1], F32)
         nc.vector.memset(one[:], 1.0)
         warm = keep.tile([P, 1], F32)
         nc.scalar.activation(out=warm[:], in_=one[:], func=ACT.Abs_reciprocal_sqrt)
 
-        w_squares = keep.tile([P, L, ROWS, P], BF16)
-        w_sumsq = keep.tile([P, L, ROWS // RUN], F32)
-        w_rsqrt = keep.tile([P, L], F32)
+        w_squares = keep.tile([P, L, 2, BLOCKS, P], BF16)
+        w_sumsq = keep.tile([P, L, 2], F32)
+        w_rsqrt = keep.tile([P, L, D], F32)
+        w_rsqrt_column = keep.tile([P, L], F32)
         nd_grouped = keep.tile([P, L, PASSES, D, PACK], BF16, align_bytes=64)
         nd_codes = keep.tile([P, L, PASSES, D], U32, align_bytes=64)
         nd_scales = keep.tile([P, L, PASSES, D], U8, align_bytes=64)
@@ -66,8 +76,8 @@ def tile_npertokenswishglu_basis_pb_s_kernel(tc, h, w_down_mix, out):
         y_sumsq = keep.tile([P, L], F32)
         y_rsqrt = keep.tile([P, L], F32)
         out_sb = keep.tile([P, L, D], F32)
-        w_rsqrt_spread = {}
-        y_banks = {}
+        w_factor = {}
+        y = {}
 
 
         def transpose_h(l):
@@ -83,40 +93,61 @@ def tile_npertokenswishglu_basis_pb_s_kernel(tc, h, w_down_mix, out):
                 nc.scalar.copy(out=grouped_words, in_=hT[:].rearrange("p g u b -> p g b u"))
 
         def sum_weight_squares(l):
-            for run in range(ROWS // RUN):
-                wT = wt_psum.tile([P, RUN, P], BF16)
-                for i in range(RUN):
-                    nc.tensor.transpose(wT[:, i, :], w_sb[:, l, run * RUN + i, :], ident_bf[:])
+            wT = wt_psum.tile([P, BLOCKS, P], F32)
+            for b in range(BLOCKS):
+                nc.tensor.transpose(wT[:, b, :], w_words[:, l, b * P : (b + 1) * P], ident_f32[:])
+            halves = wT[:].rearrange("q b p -> q (b p)").bitcast(BF16)
+            for e in range(2):
                 nc.scalar.activation(
-                    out=w_squares[:, l, run * RUN : (run + 1) * RUN],
-                    in_=wT[:],
+                    out=w_squares[:, l, e].rearrange("q b p -> q (b p)"),
+                    in_=halves[:, e::2],
                     func=ACT.Square,
-                    accum_out=w_sumsq[:, l, run : run + 1],
+                    accum_out=w_sumsq[:, l, e : e + 1],
                 )
 
-        def weight_rsqrt(l):
+        def column_weight_rsqrt(l):
+            column = scale_psum.tile([P, 1], F32, name="w_spread")
+            for e in range(2):
+                nc.tensor.matmul(
+                    column[:],
+                    lhsT=place[:, e].rearrange("q jp e -> q (jp e)"),
+                    rhs=w_sumsq[:, l, e : e + 1],
+                    start=(e == 0),
+                    stop=(e == 1),
+                )
             nc.scalar.activation(
-                out=w_rsqrt[:, l : l + 1],
-                in_=w_sumsq[:, l, 0:1],
-                func=ACT.Abs_reciprocal_sqrt,
-                bias=w_sumsq[:, l, 1:2],
+                out=w_rsqrt_column[:, l : l + 1], in_=column[:], func=ACT.Abs_reciprocal_sqrt
             )
 
         def spread_weight_rsqrt(l):
-            w_rsqrt_spread[l] = scale_psum.tile([P, D], F32, name="w_rsqrt_spread")
-            column = w_rsqrt[:, l : l + 1].to_broadcast([P, P])
-            if l < SPREAD_BY_MATMUL:
-                nc.tensor.matmul(
-                    w_rsqrt_spread[l][:], lhsT=column, rhs=ident_f32[:], start=True, stop=True
+            tile = scale_psum.tile([P, 2, PAIRS], F32, name="w_spread")
+            if l < SPREAD_BY_PRODUCT:
+                for e in range(2):
+                    nc.tensor.matmul(
+                        tile[:, e, :],
+                        lhsT=w_sumsq[:, l, e : e + 1].to_broadcast([P, P]),
+                        rhs=fold[:],
+                        start=True,
+                        stop=True,
+                    )
+                nc.scalar.activation(
+                    out=w_rsqrt[:, l].rearrange("p (jp e) -> p jp e", e=2),
+                    in_=tile[:].rearrange("p e jp -> p jp e"),
+                    func=ACT.Abs_reciprocal_sqrt,
                 )
+                w_factor[l] = w_rsqrt[:, l]
             else:
-                nc.tensor.transpose(w_rsqrt_spread[l][:], column, ident_f32[:])
+                spread = tile[:].rearrange("p e jp -> p (e jp)")
+                nc.tensor.transpose(
+                    spread, w_rsqrt_column[:, l : l + 1].to_broadcast([P, P]), ident_f32[:]
+                )
+                w_factor[l] = spread
 
         def scale_weight(l):
             for g in range(PASSES):
                 nc.vector.scalar_tensor_tensor(
                     out=nd_grouped[:, l, g],
-                    in0=w_rsqrt_spread[l][:].unsqueeze(2).to_broadcast([P, D, PACK]),
+                    in0=w_factor[l].unsqueeze(2).to_broadcast([P, D, PACK]),
                     scalar=1.0 / EPS,
                     in1=w_sb[:, l, g * PACK : (g + 1) * PACK, :].rearrange("p t j -> p j t"),
                     op0=ALU.min,
@@ -138,11 +169,19 @@ def tile_npertokenswishglu_basis_pb_s_kernel(tc, h, w_down_mix, out):
             )
 
         def multiply(l):
-            if l % BANK_TOKENS == 0:
-                y_banks[l // BANK_TOKENS] = y_psum.tile([P, BANK_TOKENS, D], F32, name="y_bank")
+            if l >= ALONE:
+                y[l] = (wt_psum.tile([P, 1, D], F32, name="wT"), 0)
+            elif l % PAIR == 0:
+                if l == ALONE - PAIR:
+                    pair = ht_psum.tile([P, PAIR, D], F32, name="hT")
+                else:
+                    pair = y_psum.tile([P, PAIR, D], F32, name="y_pair")
+                for i in range(PAIR):
+                    y[l + i] = (pair, i)
+            tile, place_in_tile = y[l]
             for g in range(PASSES):
                 nc.tensor.matmul_mx(
-                    out=y_banks[l // BANK_TOKENS][:, l % BANK_TOKENS, :],
+                    out=tile[:, place_in_tile, :],
                     lhsT=h_codes[:, l, g, :].bitcast(FP8X4),
                     lhsT_scale=h_scales[:, l, g, :],
                     rhs=nd_codes[:, l, g, :].bitcast(FP8X4),
@@ -152,9 +191,10 @@ def tile_npertokenswishglu_basis_pb_s_kernel(tc, h, w_down_mix, out):
                 )
 
         def sum_row_squares(l):
+            tile, place_in_tile = y[l]
             nc.scalar.activation(
                 out=y_squares[:, l, :],
-                in_=y_banks[l // BANK_TOKENS][:, l % BANK_TOKENS, :],
+                in_=tile[:, place_in_tile, :],
                 func=ACT.Square,
                 accum_out=y_sumsq[:, l : l + 1],
             )
@@ -164,14 +204,13 @@ def tile_npertokenswishglu_basis_pb_s_kernel(tc, h, w_down_mix, out):
                 out=y_rsqrt[:, ls], in_=y_sumsq[:, ls], func=ACT.Abs_reciprocal_sqrt
             )
 
-        def normalise_and_store(first):
-            ls = slice(first, first + PAIR)
-            in_bank = first % BANK_TOKENS
+        def normalise_and_store(ls):
+            tile = y[ls.start][0]
             nc.vector.scalar_tensor_tensor(
                 out=out_sb[:, ls, :],
-                in0=y_rsqrt[:, ls].unsqueeze(2).to_broadcast([P, PAIR, D]),
+                in0=y_rsqrt[:, ls].unsqueeze(2).to_broadcast([P, ls.stop - ls.start, D]),
                 scalar=1.0 / EPS,
-                in1=y_banks[first // BANK_TOKENS][:, in_bank : in_bank + PAIR, :],
+                in1=tile[:],
                 op0=ALU.min,
                 op1=ALU.mult,
             )
@@ -181,29 +220,34 @@ def tile_npertokenswishglu_basis_pb_s_kernel(tc, h, w_down_mix, out):
             if 0 <= l < L:
                 stage(l)
 
-        def when_pair_complete(stage, l):
-            if 0 <= l < L and l % PAIR == PAIR - 1:
-                stage(l)
+        def ends_pair(l):
+            return 0 <= l < ALONE and l % PAIR == PAIR - 1
 
-        def multiply_pair(l):
-            multiply(l - 1)
-            multiply(l)
+        def pair_of(l):
+            return slice(l - PAIR + 1, l + 1)
 
-        def row_rsqrt_pair(l):
-            row_rsqrt(slice(l - 1, l + 1))
-
-        def normalise_and_store_pair(l):
-            normalise_and_store(l - 1)
-
-        for step in range(L + 9):
+        for step in range(L + 2):
             when_in_range(spread_weight_rsqrt, step - 2)
+            if SPREAD_BY_PRODUCT <= step - 1 < L:
+                column_weight_rsqrt(step - 1)
             when_in_range(sum_weight_squares, step)
             when_in_range(transpose_h, step)
-            when_in_range(weight_rsqrt, step)
-            when_pair_complete(row_rsqrt_pair, step - 6)
+            if ends_pair(step - 6):
+                row_rsqrt(pair_of(step - 6))
             when_in_range(scale_weight, step - 2)
             when_in_range(quantise_h, step - 1)
             when_in_range(quantise_nd, step - 2)
-            when_pair_complete(multiply_pair, step - 4)
+            if ends_pair(step - 4):
+                multiply(step - 5)
+                multiply(step - 4)
             when_in_range(sum_row_squares, step - 5)
-            when_pair_complete(normalise_and_store_pair, step - 8)
+        sum_row_squares(ALONE - 1)
+        row_rsqrt(pair_of(ALONE - 1))
+        for l in range(ALONE, L):
+            multiply(l)
+            sum_row_squares(l)
+            row_rsqrt(slice(l, l + 1))
+        for l in range(PAIR - 1, ALONE, PAIR):
+            normalise_and_store(pair_of(l))
+        for l in range(ALONE, L):
+            normalise_and_store(slice(l, l + 1))

import concourse.mybir as mybir
from concourse.masks import make_identity

F32 = mybir.dt.float32
BF16 = mybir.dt.bfloat16
U32 = mybir.dt.uint32
U8 = mybir.dt.uint8
FP8X4 = mybir.dt.float8_e4m3fn_x4
ACT = mybir.ActivationFunctionType
ALU = mybir.AluOpType

P = 128
B, L, F, D = 128, 8, 1024, 128
PACK = 4
PASSES = F // (P * PACK)
ROWS = F // P
HALVES = 2
EPS = 1e-12

FLOPS = 2 * B * L * F * D

H_COPIES_ON_VECTOR = 2
SPREAD_BY_PRODUCT = 6
PAIR = 2
ALONE = L - PAIR
PAIRS = D // 2
BLOCKS = ROWS // 2


def tile_npertokenswishglu_basis_pb_s_kernel(tc, h, w_down_mix, out):
    nc = tc.nc
    with tc.tile_pool(name="keep", bufs=1) as keep, tc.psum_pool(
        name="wt_psum", bufs=2
    ) as wt_psum, tc.psum_pool(name="ht_psum", bufs=2) as ht_psum, tc.psum_pool(
        name="scale_psum", bufs=2
    ) as scale_psum, tc.psum_pool(name="y_psum", bufs=2) as y_psum, tc.manual_schedule():
        w_sb = keep.tile([P, L, ROWS, D], BF16)
        h_sb = keep.tile([P, L, F], BF16)
        for l in range(L):
            nc.sync.dma_start(
                out=w_sb[:, l].rearrange("p (g t) j -> p g (t j)", t=PACK),
                in_=w_down_mix[l].rearrange("(g p t) j -> p g (t j)", p=P, t=PACK),
            )
            nc.sync.dma_start(out=h_sb[:, l, :], in_=h[:, l, :])
        h_words = h_sb[:].bitcast(F32)

        w_words = w_sb[:].rearrange("p l r j -> p l (r j)").bitcast(F32)

        ident_f32 = keep.tile([P, P], F32)
        make_identity(nc, ident_f32[:])
        fold = keep.tile([P, PAIRS], F32)
        nc.vector.tensor_tensor(
            out=fold[:], in0=ident_f32[:, :PAIRS], in1=ident_f32[:, PAIRS:], op=ALU.add
        )
        place = keep.tile([P, 2, PAIRS, 2], F32)
        nc.vector.memset(place[:], 0.0)
        for e in range(2):
            nc.vector.tensor_copy(out=place[:, e, :, e], in_=fold[:])

        one = keep.tile([P, 1], F32)
        nc.vector.memset(one[:], 1.0)
        warm = keep.tile([P, 1], F32)
        nc.scalar.activation(out=warm[:], in_=one[:], func=ACT.Abs_reciprocal_sqrt)

        w_squares = keep.tile([P, L, 2, BLOCKS, P], BF16)
        w_sumsq = keep.tile([P, L, 2], F32)
        w_rsqrt = keep.tile([P, L, D], F32)
        w_rsqrt_column = keep.tile([P, L], F32)
        nd_grouped = keep.tile([P, L, PASSES, D, PACK], BF16, align_bytes=64)
        nd_codes = keep.tile([P, L, PASSES, D], U32, align_bytes=64)
        nd_scales = keep.tile([P, L, PASSES, D], U8, align_bytes=64)
        h_grouped = keep.tile([P, L, PASSES, B, PACK], BF16, align_bytes=64)
        h_codes = keep.tile([P, L, PASSES, B], U32, align_bytes=64)
        h_scales = keep.tile([P, L, PASSES, B], U8, align_bytes=64)
        y_squares = keep.tile([P, L, D], F32)
        y_sumsq = keep.tile([P, L], F32)
        y_rsqrt = keep.tile([P, L], F32)
        out_sb = keep.tile([P, L, D], F32)
        w_factor = {}
        y = {}


        def transpose_h(l):
            hT = ht_psum.tile([P, PASSES, HALVES, B], F32)
            for g in range(PASSES):
                for u in range(HALVES):
                    words = h_words[:, l, g * HALVES * P + u : (g + 1) * HALVES * P : HALVES]
                    nc.tensor.transpose(hT[:, g, u, :], words, ident_f32[:])
            grouped_words = h_grouped[:, l].bitcast(F32)
            if l < H_COPIES_ON_VECTOR:
                nc.vector.tensor_copy(out=grouped_words, in_=hT[:].rearrange("p g u b -> p g b u"))
            else:
                nc.scalar.copy(out=grouped_words, in_=hT[:].rearrange("p g u b -> p g b u"))

        def sum_weight_squares(l):
            wT = wt_psum.tile([P, BLOCKS, P], F32)
            for b in range(BLOCKS):
                nc.tensor.transpose(wT[:, b, :], w_words[:, l, b * P : (b + 1) * P], ident_f32[:])
            halves = wT[:].rearrange("q b p -> q (b p)").bitcast(BF16)
            for e in range(2):
                nc.scalar.activation(
                    out=w_squares[:, l, e].rearrange("q b p -> q (b p)"),
                    in_=halves[:, e::2],
                    func=ACT.Square,
                    accum_out=w_sumsq[:, l, e : e + 1],
                )

        def column_weight_rsqrt(l):
            column = scale_psum.tile([P, 1], F32, name="w_spread")
            for e in range(2):
                nc.tensor.matmul(
                    column[:],
                    lhsT=place[:, e].rearrange("q jp e -> q (jp e)"),
                    rhs=w_sumsq[:, l, e : e + 1],
                    start=(e == 0),
                    stop=(e == 1),
                )
            nc.scalar.activation(
                out=w_rsqrt_column[:, l : l + 1], in_=column[:], func=ACT.Abs_reciprocal_sqrt
            )

        def spread_weight_rsqrt(l):
            tile = scale_psum.tile([P, 2, PAIRS], F32, name="w_spread")
            if l < SPREAD_BY_PRODUCT:
                for e in range(2):
                    nc.tensor.matmul(
                        tile[:, e, :],
                        lhsT=w_sumsq[:, l, e : e + 1].to_broadcast([P, P]),
                        rhs=fold[:],
                        start=True,
                        stop=True,
                    )
                nc.scalar.activation(
                    out=w_rsqrt[:, l].rearrange("p (jp e) -> p jp e", e=2),
                    in_=tile[:].rearrange("p e jp -> p jp e"),
                    func=ACT.Abs_reciprocal_sqrt,
                )
                w_factor[l] = w_rsqrt[:, l]
            else:
                spread = tile[:].rearrange("p e jp -> p (e jp)")
                nc.tensor.transpose(
                    spread, w_rsqrt_column[:, l : l + 1].to_broadcast([P, P]), ident_f32[:]
                )
                w_factor[l] = spread

        def scale_weight(l):
            for g in range(PASSES):
                nc.vector.scalar_tensor_tensor(
                    out=nd_grouped[:, l, g],
                    in0=w_factor[l].unsqueeze(2).to_broadcast([P, D, PACK]),
                    scalar=1.0 / EPS,
                    in1=w_sb[:, l, g * PACK : (g + 1) * PACK, :].rearrange("p t j -> p j t"),
                    op0=ALU.min,
                    op1=ALU.mult,
                )

        def quantise_h(l):
            nc.vector.quantize_mx(
                out=h_codes[:, l].rearrange("p g b -> p (g b)").bitcast(FP8X4),
                scales=h_scales[:, l].rearrange("p g b -> p (g b)"),
                in_=h_grouped[:, l].rearrange("p g b t -> p (g b t)"),
            )

        def quantise_nd(l):
            nc.vector.quantize_mx(
                out=nd_codes[:, l].rearrange("p g j -> p (g j)").bitcast(FP8X4),
                scales=nd_scales[:, l].rearrange("p g j -> p (g j)"),
                in_=nd_grouped[:, l].rearrange("p g j t -> p (g j t)"),
            )

        def multiply(l):
            if l >= ALONE:
                y[l] = (wt_psum.tile([P, 1, D], F32, name="wT"), 0)
            elif l % PAIR == 0:
                if l == ALONE - PAIR:
                    pair = ht_psum.tile([P, PAIR, D], F32, name="hT")
                else:
                    pair = y_psum.tile([P, PAIR, D], F32, name="y_pair")
                for i in range(PAIR):
                    y[l + i] = (pair, i)
            tile, place_in_tile = y[l]
            for g in range(PASSES):
                nc.tensor.matmul_mx(
                    out=tile[:, place_in_tile, :],
                    lhsT=h_codes[:, l, g, :].bitcast(FP8X4),
                    lhsT_scale=h_scales[:, l, g, :],
                    rhs=nd_codes[:, l, g, :].bitcast(FP8X4),
                    rhs_scale=nd_scales[:, l, g, :],
                    start=(g == 0),
                    stop=(g == PASSES - 1),
                )

        def sum_row_squares(l):
            tile, place_in_tile = y[l]
            nc.scalar.activation(
                out=y_squares[:, l, :],
                in_=tile[:, place_in_tile, :],
                func=ACT.Square,
                accum_out=y_sumsq[:, l : l + 1],
            )

        def row_rsqrt(ls):
            nc.scalar.activation(
                out=y_rsqrt[:, ls], in_=y_sumsq[:, ls], func=ACT.Abs_reciprocal_sqrt
            )

        def normalise_and_store(ls):
            tile = y[ls.start][0]
            nc.vector.scalar_tensor_tensor(
                out=out_sb[:, ls, :],
                in0=y_rsqrt[:, ls].unsqueeze(2).to_broadcast([P, ls.stop - ls.start, D]),
                scalar=1.0 / EPS,
                in1=tile[:],
                op0=ALU.min,
                op1=ALU.mult,
            )
            nc.sync.dma_start(out=out[:, ls, :], in_=out_sb[:, ls, :])

        def when_in_range(stage, l):
            if 0 <= l < L:
                stage(l)

        def ends_pair(l):
            return 0 <= l < ALONE and l % PAIR == PAIR - 1

        def pair_of(l):
            return slice(l - PAIR + 1, l + 1)

        for step in range(L + 2):
            when_in_range(spread_weight_rsqrt, step - 2)
            if SPREAD_BY_PRODUCT <= step - 1 < L:
                column_weight_rsqrt(step - 1)
            when_in_range(sum_weight_squares, step)
            when_in_range(transpose_h, step)
            if ends_pair(step - 6):
                row_rsqrt(pair_of(step - 6))
            when_in_range(scale_weight, step - 2)
            when_in_range(quantise_h, step - 1)
            when_in_range(quantise_nd, step - 2)
            if ends_pair(step - 4):
                multiply(step - 5)
                multiply(step - 4)
            when_in_range(sum_row_squares, step - 5)
        sum_row_squares(ALONE - 1)
        row_rsqrt(pair_of(ALONE - 1))
        for l in range(ALONE, L):
            multiply(l)
            sum_row_squares(l)
            row_rsqrt(slice(l, l + 1))
        for l in range(PAIR - 1, ALONE, PAIR):
            normalise_and_store(pair_of(l))
        for l in range(ALONE, L):
            normalise_and_store(slice(l, l + 1))
